import numpy as np
import ml_dtypes


def mxq(x, axis, fmt="e4m3"):
    dtype, down = {"e4m3": (ml_dtypes.float8_e4m3fn, 7), "e5m2": (ml_dtypes.float8_e5m2, 14)}[fmt]
    v = np.moveaxis(np.asarray(x, np.float32).astype(ml_dtypes.bfloat16).astype(np.float64), axis, -1)
    blocks = v.reshape(v.shape[:-1] + (-1, 32))
    amax = np.abs(blocks).max(-1, keepdims=True)
    byte = np.maximum(np.where(amax > 0, np.frexp(amax)[1] - 1 + 127, 0) - down, 1)
    scale = np.exp2(byte - 127.0)
    codes = (blocks / scale).astype(np.float32).astype(dtype).astype(np.float64)
    return np.moveaxis((codes * scale).reshape(v.shape), -1, axis)


WIDE = False


def mx_kscale(k):
    if not WIDE:
        return np.ones(k)
    levels = np.array([10, -10, 5, -5, 0])
    a = np.random.permutation(np.resize(levels, k // 512 * 4)).reshape(k // 512, 4)
    idx = np.arange(k)
    return np.exp2(a[idx // 512, idx % 128 // 32])


BF16 = ml_dtypes.bfloat16


def bf(x):
    return np.asarray(x, np.float32).astype(BF16)


def f64(x):
    return np.asarray(x).astype(np.float64)


B, C, T, E, H = 1, 512, 4, 1024, 8
D = E // H
S = C * T


def heads(y):
    return np.moveaxis(y.reshape(B, C, T, H, D), 3, 1)


def setup_inputs():
    s = mx_kscale(E)
    return {"hidden_states": bf(np.random.standard_normal((B, S, E)) * s),
            "wk": bf(np.random.standard_normal((E, E)) * 2.0 / np.sqrt(E) / s[None, :]),
            "bk": bf(np.random.standard_normal(E) * 0.3),
            "wv": bf(np.random.standard_normal((E, E)) * 2.0 / np.sqrt(E) / s[None, :]),
            "bv": bf(np.random.standard_normal(E) * 0.3)}


def reference(hidden_states, wk, bk, wv, bv):
    xq = mxq(f64(hidden_states), 2, "e4m3")
    k = heads((xq @ mxq(f64(wk), 1, "e4m3").T) + f64(bk))
    v = heads((xq @ mxq(f64(wv), 1, "e4m3").T) + f64(bv))
    return k, v, k.mean(axis=3), v.mean(axis=3)

@@ -1,0 +1,248 @@
+from contextlib import ExitStack
+
+import concourse.mybir as mybir
+from concourse.masks import make_identity
+
+F32 = mybir.dt.float32
+BF16 = mybir.dt.bfloat16
+U32 = mybir.dt.uint32
+U8 = mybir.dt.uint8
+FP8X4 = mybir.dt.float8_e4m3fn_x4
+ADD = mybir.AluOpType.add
+MULT = mybir.AluOpType.mult
+COPY = mybir.ActivationFunctionType.Copy
+
+FLOPS = 2 * 2048 * 1024 * 2048
+
+P = 128
+UNITS = (("w", 0), ("x", 0), ("x", 1), ("x", 2), ("x", 3), ("w", 1), ("w", 2), ("w", 3))
+LOAD_PIECES = (2, 4, 4, 1, 1, 1, 1, 1)
+QUANT_PIECES = (2, 4, 4, 1, 1, 1, 1, 1)
+VECTOR_BANKS = ((1, 3), (), (), (), (), (), (), ())
+PROLOGUE = (
+    ("L", 0), ("L", 1), ("L", 2), ("L", 3), ("B", 0, "s"), ("B", 1, "v"), ("T", 0), ("L", 4), ("Qp", 0, 0),
+    ("Tb", 1, 0), ("Qp", 1, 0), ("Qp", 0, 1), ("Tb", 1, 1), ("Qp", 1, 1), ("Tb", 1, 2), ("Qp", 1, 2), ("Tb", 1, 3),
+    ("Qp", 1, 3), ("L", 5),
+)
+AFTER = {
+    0: (("T", 2), ("L", 6), ("Q", 2), ("T", 3), ("L", 7)),
+    1: (("T", 4), ("B", 2, "s"), ("B", 3, "s")),
+    2: (("T", 5),),
+}
+PE_IN = {
+    (3, 3): (("Tb", 6, 0), ("Tb", 6, 1)), (4, 3): (("Tb", 6, 2), ("Tb", 6, 3)),
+    (7, 3): (("Tb", 7, 0), ("Tb", 7, 1)), (8, 3): (("Tb", 7, 2), ("Tb", 7, 3)),
+}
+V_IN = {(1, 1): (("Q", 3),), (2, 1): (("Q", 4),), (3, 1): (("Q", 5),), (5, 3): (("Q", 6),), (9, 3): (("Q", 7),)}
+V_SUM = (9, 12, 15)
+SCALE_LAG = 2
+
+
+def tile_chunkedattention_pb_kernel(tc, hidden_states, wk, bk, wv, bv, out_0, out_1, out_2, out_3):
+    nc = tc.nc
+    x_view = hidden_states.flatten_outer_dims().rearrange("(p q t) e -> p q (t e)", p=P, q=4, t=4)
+    w_views = [w.rearrange("(n f p) e -> p n f e", n=2, f=4, p=P) for w in (wk, wv)]
+    kv_views = [o.rearrange("b h (p q) t d -> p (b h) (q t d)", p=P, q=4) for o in (out_0, out_1)]
+    mean_views = [o.rearrange("b h (p q) d -> p (b h) (q d)", p=P, q=4) for o in (out_2, out_3)]
+
+    with ExitStack() as ctx:
+        const = ctx.enter_context(tc.tile_pool(name="const", bufs=1))
+        rawp = ctx.enter_context(tc.tile_pool(name="rawp", bufs=4))
+        grp = ctx.enter_context(tc.tile_pool(name="grp", bufs=3))
+        outp = ctx.enter_context(tc.tile_pool(name="outp", bufs=5))
+        halfp = ctx.enter_context(tc.tile_pool(name="halfp", bufs=2))
+        totalp = ctx.enter_context(tc.tile_pool(name="totalp", bufs=4))
+        meanp = ctx.enter_context(tc.tile_pool(name="meanp", bufs=2))
+        psum_t = ctx.enter_context(tc.psum_pool(name="psum_t", bufs=4))
+        psum_m = ctx.enter_context(tc.psum_pool(name="psum_m", bufs=4))
+        ctx.enter_context(tc.manual_schedule())
+
+        ident = const.tile([P, P], F32)
+        make_identity(nc, ident[:])
+        ones = const.tile([P, P], BF16)
+        nc.vector.memset(ones[:], 1.0)
+        brow = const.tile([P, 2048], BF16)
+        nc.vector.memset(brow[:], 0.0)
+        nc.scalar.dma_start(out=brow[0:1, 0:1024], in_=bk.unsqueeze(0))
+        nc.scalar.dma_start(out=brow[0:1, 1024:2048], in_=bv.unsqueeze(0))
+        bias_sb = const.tile([P, 2048], F32)
+        xc = const.tile([P, 4096], U32, align_bytes=64)
+        xs = const.tile([P, 4096], U8, align_bytes=64)
+        wc = const.tile([P, 4096], U32, align_bytes=64)
+        ws = const.tile([P, 4096], U8, align_bytes=64)
+
+        raws = {}
+        groupeds = {}
+
+        def load(u):
+            kind, i = UNITS[u]
+            pieces = LOAD_PIECES[u]
+            raw = rawp.tile([P, 4096], BF16)
+            if kind == "x":
+                w = 4096 // pieces
+                for c in range(pieces):
+                    nc.sync.dma_start(out=raw[:, c * w:(c + 1) * w], in_=x_view[:, i, c * w:(c + 1) * w])
+            else:
+                dst = raw[:].rearrange("p (f e) -> p f e", f=4)
+                k = 4 // pieces
+                for c in range(pieces):
+                    nc.sync.dma_start(out=dst[:, c * k:(c + 1) * k, :], in_=w_views[i // 2][:, i % 2, c * k:(c + 1) * k, :])
+            raws[u] = raw
+
+        def transpose_bank(u, b):
+            kind = UNITS[u][0]
+            if b == 0:
+                grouped = grp.tile([P, 4096], BF16, align_bytes=64)
+                groupeds[u] = grouped
+            raw32 = raws[u][:].bitcast(F32)
+            g32 = groupeds[u][:].bitcast(F32)
+            if kind == "x":
+                dst = g32.rearrange("p (b s c u) -> p b s c u", b=4, s=2, c=P, u=2)
+            else:
+                dst = g32.rearrange("p (s b c u) -> p b s c u", s=2, b=4, c=P, u=2)
+            tp = psum_t.tile([P, 512], F32)
+            for a in range(4):
+                lo = 512 * b + P * a
+                nc.tensor.transpose(tp[:, P * a:P * (a + 1)], raw32[:, lo:lo + P], ident[:])
+            src = tp[:].rearrange("p (s u c) -> p s c u", s=2, u=2, c=P)
+            if b in VECTOR_BANKS[u]:
+                nc.vector.tensor_copy(out=dst[:, b], in_=src)
+            else:
+                nc.scalar.copy(out=dst[:, b], in_=src)
+
+        def quantise_piece(u, c):
+            kind, i = UNITS[u]
+            codes, scales = (xc, xs) if kind == "x" else (wc, ws)
+            w = 1024 // QUANT_PIECES[u]
+            lo = 1024 * i + c * w
+            nc.vector.quantize_mx(
+                out=codes[:, lo:lo + w].bitcast(FP8X4),
+                scales=scales[:, lo:lo + w],
+                in_=groupeds[u][:, 4 * c * w:4 * (c + 1) * w],
+            )
+
+        def bias_block(n, eng):
+            acc = psum_m.tile([P, 512], F32)
+            nc.tensor.matmul(out=acc[:], lhsT=ones[:], rhs=brow[:, 512 * n:512 * (n + 1)], start=True, stop=True)
+            if eng == "v":
+                nc.vector.tensor_copy(out=bias_sb[:, 512 * n:512 * (n + 1)], in_=acc[:])
+            else:
+                nc.scalar.copy(out=bias_sb[:, 512 * n:512 * (n + 1)], in_=acc[:])
+
+        def run_ops(ops):
+            for op in ops:
+                if op[0] == "L":
+                    load(op[1])
+                elif op[0] == "T":
+                    for b in range(4):
+                        transpose_bank(op[1], b)
+                elif op[0] == "Tb":
+                    transpose_bank(op[1], op[2])
+                elif op[0] == "Q":
+                    for c in range(QUANT_PIECES[op[1]]):
+                        quantise_piece(op[1], c)
+                elif op[0] == "Qp":
+                    quantise_piece(op[1], op[2])
+                else:
+                    bias_block(op[1], op[2])
+
+        run_ops(PROLOGUE)
+
+        o_tiles = {}
+        totals = {}
+        m_tiles = {}
+
+        def mean_tile(n):
+            if n not in m_tiles:
+                m = meanp.tile([P, 4, 4, P], F32)
+                m_tiles[n] = m
+            return m_tiles[n]
+
+        def store_means(n, q0, q1):
+            m = m_tiles[n]
+            h0 = 4 * (n % 2)
+            nc.scalar.dma_start(
+                out=mean_views[n // 2][:, h0:h0 + 4, P * q0:P * q1],
+                in_=m[:, :, q0:q1, :].rearrange("p h q d -> p h (q d)"),
+            )
+
+        def after_mean(r):
+            n, q = divmod(r, 4)
+            if n == 3:
+                if q == 2:
+                    store_means(n, 0, 3)
+                if q == 3:
+                    store_means(n, 3, 4)
+            elif q == 3:
+                store_means(n, 0, 4)
+
+        def scale_round(r):
+            n, q = divmod(r, 4)
+            m = mean_tile(n)
+            nc.scalar.activation(out=m[:, :, q, :], in_=totals[r][:], func=COPY, scale=0.25)
+            after_mean(r)
+
+        pending = []
+        for r in range(16):
+            n, q = divmod(r, 4)
+            g = q % 2
+            banks = []
+            for j in range(4):
+                acc = psum_m.tile([P, 512], F32)
+                for s in range(2):
+                    xo = 1024 * q + 256 * j + P * s
+                    wo = 1024 * n + 512 * s
+                    nc.tensor.matmul_mx(
+                        out=acc[:],
+                        lhsT=xc[:, xo:xo + P].bitcast(FP8X4),
+                        lhsT_scale=xs[:, xo:xo + P],
+                        rhs=wc[:, wo:wo + 512].bitcast(FP8X4),
+                        rhs_scale=ws[:, wo:wo + 512],
+                        start=(s == 0),
+                        stop=(s == 1),
+                    )
+                banks.append(acc)
+                run_ops(PE_IN.get((r, j), ()))
+            if g == 0:
+                o = outp.tile([P, 4, 8, P], F32)
+                o_tiles[r // 2] = o
+            o = o_tiles[r // 2]
+            bias_v = bias_sb[:, 512 * n:512 * (n + 1)].rearrange("p (h d) -> p h d", h=4)
+            if r in V_SUM:
+                run = totalp.tile([P, 4, P], F32, tag="total")
+            for j in range(4):
+                bank_v = banks[j][:].rearrange("p (h d) -> p h d", h=4)
+                nc.vector.tensor_tensor(out=o[:, :, 4 * g + j, :], in0=bank_v, in1=bias_v, op=ADD)
+                if r in V_SUM:
+                    dst = mean_tile(n)[:, :, q, :] if j == 3 else run[:]
+                    nc.vector.scalar_tensor_tensor(
+                        out=dst, in0=bank_v, scalar=0.25, in1=(bias_v if j == 0 else run[:]), op0=MULT, op1=ADD
+                    )
+                run_ops(V_IN.get((r, j), ()))
+            run_ops(AFTER.get(r, ()))
+            h0 = 4 * (n % 2)
+            if r >= 14:
+                nc.sync.dma_start(
+                    out=kv_views[n // 2][:, h0:h0 + 4, 512 * q:512 * (q + 1)],
+                    in_=o[:, :, 4 * g:4 * (g + 1), :].rearrange("p h j d -> p h (j d)"),
+                )
+            elif g == 1:
+                nc.sync.dma_start(
+                    out=kv_views[n // 2][:, h0:h0 + 4, 512 * (q - 1):512 * (q + 1)],
+                    in_=o[:].rearrange("p h j d -> p h (j d)"),
+                )
+            if r in V_SUM:
+                pending.append((r, r, "stored"))
+            else:
+                half = halfp.tile([P, 4, 2, P], F32)
+                nc.gpsimd.tensor_tensor(out=half[:], in0=o[:, :, 4 * g:4 * g + 2, :], in1=o[:, :, 4 * g + 2:4 * g + 4, :], op=ADD)
+                total = totalp.tile([P, 4, P], F32, tag="total")
+                nc.gpsimd.tensor_tensor(out=total[:], in0=half[:, :, 0, :], in1=half[:, :, 1, :], op=ADD)
+                totals[r] = total
+                pending.append((min(15, r + SCALE_LAG), r, "scale"))
+            for due, rr, what in sorted(pending, key=lambda item: item[1]):
+                if due == r:
+                    if what == "scale":
+                        scale_round(rr)
+                    else:
+                        after_mean(rr)

@@ -15,27 +15,11 @@ COPY = mybir.ActivationFunctionType.Copy
 FLOPS = 2 * 2048 * 1024 * 2048
 
 P = 128
-UNITS = (("w", 0), ("x", 0), ("x", 1), ("x", 2), ("x", 3), ("w", 1), ("w", 2), ("w", 3))
-LOAD_PIECES = (2, 4, 4, 1, 1, 1, 1, 1)
-QUANT_PIECES = (2, 4, 4, 1, 1, 1, 1, 1)
-VECTOR_BANKS = ((1, 3), (), (), (), (), (), (), ())
-PROLOGUE = (
-    ("L", 0), ("L", 1), ("L", 2), ("L", 3), ("B", 0, "s"), ("B", 1, "v"), ("T", 0), ("L", 4), ("Qp", 0, 0),
-    ("Tb", 1, 0), ("Qp", 1, 0), ("Qp", 0, 1), ("Tb", 1, 1), ("Qp", 1, 1), ("Tb", 1, 2), ("Qp", 1, 2), ("Tb", 1, 3),
-    ("Qp", 1, 3), ("L", 5),
-)
-AFTER = {
-    0: (("T", 2), ("L", 6), ("Q", 2), ("T", 3), ("L", 7)),
-    1: (("T", 4), ("B", 2, "s"), ("B", 3, "s")),
-    2: (("T", 5),),
-}
-PE_IN = {
-    (3, 3): (("Tb", 6, 0), ("Tb", 6, 1)), (4, 3): (("Tb", 6, 2), ("Tb", 6, 3)),
-    (7, 3): (("Tb", 7, 0), ("Tb", 7, 1)), (8, 3): (("Tb", 7, 2), ("Tb", 7, 3)),
-}
-V_IN = {(1, 1): (("Q", 3),), (2, 1): (("Q", 4),), (3, 1): (("Q", 5),), (5, 3): (("Q", 6),), (9, 3): (("Q", 7),)}
-V_SUM = (9, 12, 15)
-SCALE_LAG = 2
+BANK = 512
+UNIT = 4096
+WORDS = UNIT // 4
+ROUNDS = 16
+SCALE_LAG = 3
 
 
 def tile_chunkedattention_pb_kernel(tc, hidden_states, wk, bk, wv, bv, out_0, out_1, out_2, out_3):
@@ -45,14 +29,24 @@ def tile_chunkedattention_pb_kernel(tc, hidden_states, wk, bk, wv, bv, out_0, ou
     kv_views = [o.rearrange("b h (p q) t d -> p (b h) (q t d)", p=P, q=4) for o in (out_0, out_1)]
     mean_views = [o.rearrange("b h (p q) d -> p (b h) (q d)", p=P, q=4) for o in (out_2, out_3)]
 
+    units = [("w", 0), ("x", 0), ("x", 1), ("x", 2), ("x", 3), ("w", 1), ("w", 2), ("w", 3)]
+
+    def first_round(unit):
+        kind, i = unit
+        return i if kind == "x" else 4 * i
+
+    def summed_on_vector(r):
+        return r % 4 == 3 and r > 3
+
     with ExitStack() as ctx:
         const = ctx.enter_context(tc.tile_pool(name="const", bufs=1))
-        rawp = ctx.enter_context(tc.tile_pool(name="rawp", bufs=4))
-        grp = ctx.enter_context(tc.tile_pool(name="grp", bufs=3))
-        outp = ctx.enter_context(tc.tile_pool(name="outp", bufs=5))
-        halfp = ctx.enter_context(tc.tile_pool(name="halfp", bufs=2))
-        totalp = ctx.enter_context(tc.tile_pool(name="totalp", bufs=4))
-        meanp = ctx.enter_context(tc.tile_pool(name="meanp", bufs=2))
+        raw_pool = ctx.enter_context(tc.tile_pool(name="raw_pool", bufs=4))
+        grouped_pool = ctx.enter_context(tc.tile_pool(name="grouped_pool", bufs=3))
+        out_pool = ctx.enter_context(tc.tile_pool(name="out_pool", bufs=8))
+        half_pool = ctx.enter_context(tc.tile_pool(name="half_pool", bufs=2))
+        total_pool = ctx.enter_context(tc.tile_pool(name="total_pool", bufs=SCALE_LAG + 2))
+        run_pool = ctx.enter_context(tc.tile_pool(name="run_pool", bufs=2))
+        mean_pool = ctx.enter_context(tc.tile_pool(name="mean_pool", bufs=2))
         psum_t = ctx.enter_context(tc.psum_pool(name="psum_t", bufs=4))
         psum_m = ctx.enter_context(tc.psum_pool(name="psum_m", bufs=4))
         ctx.enter_context(tc.manual_schedule())
@@ -61,188 +55,150 @@ def tile_chunkedattention_pb_kernel(tc, hidden_states, wk, bk, wv, bv, out_0, ou
         make_identity(nc, ident[:])
         ones = const.tile([P, P], BF16)
         nc.vector.memset(ones[:], 1.0)
-        brow = const.tile([P, 2048], BF16)
-        nc.vector.memset(brow[:], 0.0)
-        nc.scalar.dma_start(out=brow[0:1, 0:1024], in_=bk.unsqueeze(0))
-        nc.scalar.dma_start(out=brow[0:1, 1024:2048], in_=bv.unsqueeze(0))
-        bias_sb = const.tile([P, 2048], F32)
-        xc = const.tile([P, 4096], U32, align_bytes=64)
-        xs = const.tile([P, 4096], U8, align_bytes=64)
-        wc = const.tile([P, 4096], U32, align_bytes=64)
-        ws = const.tile([P, 4096], U8, align_bytes=64)
-
+        bias_rows = const.tile([P, 4 * BANK], BF16)
+        nc.vector.memset(bias_rows[:], 0.0)
+        nc.scalar.dma_start(out=bias_rows[0:1, 0:2 * BANK], in_=bk.unsqueeze(0))
+        nc.scalar.dma_start(out=bias_rows[0:1, 2 * BANK:4 * BANK], in_=bv.unsqueeze(0))
+        bias = const.tile([P, 4 * BANK], F32)
+        codes = {
+            "x": const.tile([P, 4 * WORDS], U32, align_bytes=64, name="x_codes"),
+            "w": const.tile([P, 4 * WORDS], U32, align_bytes=64, name="w_codes"),
+        }
+        scales = {
+            "x": const.tile([P, 4 * WORDS], U8, align_bytes=64, name="x_scales"),
+            "w": const.tile([P, 4 * WORDS], U8, align_bytes=64, name="w_scales"),
+        }
         raws = {}
         groupeds = {}
 
-        def load(u):
-            kind, i = UNITS[u]
-            pieces = LOAD_PIECES[u]
-            raw = rawp.tile([P, 4096], BF16)
+        def load(unit, pieces):
+            kind, i = unit
+            raw = raw_pool.tile([P, UNIT], BF16)
             if kind == "x":
-                w = 4096 // pieces
-                for c in range(pieces):
-                    nc.sync.dma_start(out=raw[:, c * w:(c + 1) * w], in_=x_view[:, i, c * w:(c + 1) * w])
+                src = x_view[:, i, :].rearrange("p (f e) -> p f e", f=4)
             else:
-                dst = raw[:].rearrange("p (f e) -> p f e", f=4)
-                k = 4 // pieces
-                for c in range(pieces):
-                    nc.sync.dma_start(out=dst[:, c * k:(c + 1) * k, :], in_=w_views[i // 2][:, i % 2, c * k:(c + 1) * k, :])
-            raws[u] = raw
+                src = w_views[i // 2][:, i % 2]
+            dst = raw[:].rearrange("p (f e) -> p f e", f=4)
+            step = 4 // pieces
+            for f in range(0, 4, step):
+                nc.sync.dma_start(out=dst[:, f:f + step, :], in_=src[:, f:f + step, :])
+            raws[unit] = raw
 
-        def transpose_bank(u, b):
-            kind = UNITS[u][0]
-            if b == 0:
-                grouped = grp.tile([P, 4096], BF16, align_bytes=64)
-                groupeds[u] = grouped
-            raw32 = raws[u][:].bitcast(F32)
-            g32 = groupeds[u][:].bitcast(F32)
+        def transpose(unit, vector_helps):
+            kind = unit[0]
+            raw_words = raws[unit][:].bitcast(F32)
+            grouped = grouped_pool.tile([P, UNIT], BF16, align_bytes=64)
+            grouped_words = grouped[:].bitcast(F32)
             if kind == "x":
-                dst = g32.rearrange("p (b s c u) -> p b s c u", b=4, s=2, c=P, u=2)
+                dst = grouped_words.rearrange("p (f s c u) -> p f s c u", f=4, s=2, c=P, u=2)
             else:
-                dst = g32.rearrange("p (s b c u) -> p b s c u", s=2, b=4, c=P, u=2)
-            tp = psum_t.tile([P, 512], F32)
-            for a in range(4):
-                lo = 512 * b + P * a
-                nc.tensor.transpose(tp[:, P * a:P * (a + 1)], raw32[:, lo:lo + P], ident[:])
-            src = tp[:].rearrange("p (s u c) -> p s c u", s=2, u=2, c=P)
-            if b in VECTOR_BANKS[u]:
-                nc.vector.tensor_copy(out=dst[:, b], in_=src)
-            else:
-                nc.scalar.copy(out=dst[:, b], in_=src)
+                dst = grouped_words.rearrange("p (s f c u) -> p f s c u", s=2, f=4, c=P, u=2)
+            for f in range(4):
+                turned = psum_t.tile([P, BANK], F32)
+                for a in range(4):
+                    lo = BANK * f + P * a
+                    nc.tensor.transpose(turned[:, P * a:P * (a + 1)], raw_words[:, lo:lo + P], ident[:])
+                src = turned[:].rearrange("p (s u c) -> p s c u", s=2, u=2, c=P)
+                if vector_helps and f % 2 == 1:
+                    nc.vector.tensor_copy(out=dst[:, f], in_=src)
+                else:
+                    nc.scalar.copy(out=dst[:, f], in_=src)
+            groupeds[unit] = grouped
 
-        def quantise_piece(u, c):
-            kind, i = UNITS[u]
-            codes, scales = (xc, xs) if kind == "x" else (wc, ws)
-            w = 1024 // QUANT_PIECES[u]
-            lo = 1024 * i + c * w
+        def quantise(unit):
+            kind, i = unit
             nc.vector.quantize_mx(
-                out=codes[:, lo:lo + w].bitcast(FP8X4),
-                scales=scales[:, lo:lo + w],
-                in_=groupeds[u][:, 4 * c * w:4 * (c + 1) * w],
+                out=codes[kind][:, WORDS * i:WORDS * (i + 1)].bitcast(FP8X4),
+                scales=scales[kind][:, WORDS * i:WORDS * (i + 1)],
+                in_=groupeds[unit][:],
             )
 
-        def bias_block(n, eng):
-            acc = psum_m.tile([P, 512], F32)
-            nc.tensor.matmul(out=acc[:], lhsT=ones[:], rhs=brow[:, 512 * n:512 * (n + 1)], start=True, stop=True)
-            if eng == "v":
-                nc.vector.tensor_copy(out=bias_sb[:, 512 * n:512 * (n + 1)], in_=acc[:])
-            else:
-                nc.scalar.copy(out=bias_sb[:, 512 * n:512 * (n + 1)], in_=acc[:])
+        load(units[0], 2)
+        for unit in units[1:4]:
+            load(unit, 1)
+        for k in range(2):
+            transpose(units[k], True)
+            load(units[k + 4], 1)
+            quantise(units[k])
+        for n in range(4):
+            spread = psum_m.tile([P, BANK], F32, tag="acc")
+            nc.tensor.matmul(out=spread[:], lhsT=ones[:], rhs=bias_rows[:, BANK * n:BANK * (n + 1)], start=True, stop=True)
+            nc.vector.tensor_copy(out=bias[:, BANK * n:BANK * (n + 1)], in_=spread[:])
+        prepared = 2
 
-        def run_ops(ops):
-            for op in ops:
-                if op[0] == "L":
-                    load(op[1])
-                elif op[0] == "T":
-                    for b in range(4):
-                        transpose_bank(op[1], b)
-                elif op[0] == "Tb":
-                    transpose_bank(op[1], op[2])
-                elif op[0] == "Q":
-                    for c in range(QUANT_PIECES[op[1]]):
-                        quantise_piece(op[1], c)
-                elif op[0] == "Qp":
-                    quantise_piece(op[1], op[2])
-                else:
-                    bias_block(op[1], op[2])
-
-        run_ops(PROLOGUE)
-
-        o_tiles = {}
         totals = {}
-        m_tiles = {}
+        means = {}
 
         def mean_tile(n):
-            if n not in m_tiles:
-                m = meanp.tile([P, 4, 4, P], F32)
-                m_tiles[n] = m
-            return m_tiles[n]
+            if n not in means:
+                means[n] = mean_pool.tile([P, 4, 4, P], F32, name="mean")
+            return means[n]
 
-        def store_means(n, q0, q1):
-            m = m_tiles[n]
-            h0 = 4 * (n % 2)
-            nc.scalar.dma_start(
-                out=mean_views[n // 2][:, h0:h0 + 4, P * q0:P * q1],
-                in_=m[:, :, q0:q1, :].rearrange("p h q d -> p h (q d)"),
-            )
-
-        def after_mean(r):
+        def scale(r):
             n, q = divmod(r, 4)
-            if n == 3:
-                if q == 2:
-                    store_means(n, 0, 3)
-                if q == 3:
-                    store_means(n, 3, 4)
-            elif q == 3:
-                store_means(n, 0, 4)
+            nc.scalar.activation(out=mean_tile(n)[:, :, q, :], in_=totals[r][:], func=COPY, scale=0.25)
+            if r == max(s for s in range(4 * n, 4 * n + 4) if not summed_on_vector(s)):
+                nc.scalar.dma_start(
+                    out=mean_views[n // 2][:, 4 * (n % 2):4 * (n % 2) + 4, :],
+                    in_=means[n][:].rearrange("p h q d -> p h (q d)"),
+                )
 
-        def scale_round(r):
+        waiting = []
+        scaled = 0
+        for r in range(ROUNDS):
             n, q = divmod(r, 4)
-            m = mean_tile(n)
-            nc.scalar.activation(out=m[:, :, q, :], in_=totals[r][:], func=COPY, scale=0.25)
-            after_mean(r)
-
-        pending = []
-        for r in range(16):
-            n, q = divmod(r, 4)
-            g = q % 2
+            fresh = None
+            if prepared < len(units) and r == first_round(units[prepared - 1]):
+                fresh = units[prepared]
+                transpose(fresh, False)
+                if prepared + 4 < len(units):
+                    load(units[prepared + 4], 1)
+                prepared += 1
             banks = []
             for j in range(4):
-                acc = psum_m.tile([P, 512], F32)
+                acc = psum_m.tile([P, BANK], F32)
                 for s in range(2):
-                    xo = 1024 * q + 256 * j + P * s
-                    wo = 1024 * n + 512 * s
+                    xo = WORDS * q + 2 * P * j + P * s
+                    wo = WORDS * n + BANK * s
                     nc.tensor.matmul_mx(
                         out=acc[:],
-                        lhsT=xc[:, xo:xo + P].bitcast(FP8X4),
-                        lhsT_scale=xs[:, xo:xo + P],
-                        rhs=wc[:, wo:wo + 512].bitcast(FP8X4),
-                        rhs_scale=ws[:, wo:wo + 512],
+                        lhsT=codes["x"][:, xo:xo + P].bitcast(FP8X4),
+                        lhsT_scale=scales["x"][:, xo:xo + P],
+                        rhs=codes["w"][:, wo:wo + BANK].bitcast(FP8X4),
+                        rhs_scale=scales["w"][:, wo:wo + BANK],
                         start=(s == 0),
                         stop=(s == 1),
                     )
                 banks.append(acc)
-                run_ops(PE_IN.get((r, j), ()))
-            if g == 0:
-                o = outp.tile([P, 4, 8, P], F32)
-                o_tiles[r // 2] = o
-            o = o_tiles[r // 2]
-            bias_v = bias_sb[:, 512 * n:512 * (n + 1)].rearrange("p (h d) -> p h d", h=4)
-            if r in V_SUM:
-                run = totalp.tile([P, 4, P], F32, tag="total")
+            o = out_pool.tile([P, 4, 4, P], F32)
+            bias_n = bias[:, BANK * n:BANK * (n + 1)].rearrange("p (h d) -> p h d", h=4)
+            if summed_on_vector(r):
+                run = run_pool.tile([P, 4, P], F32)
             for j in range(4):
-                bank_v = banks[j][:].rearrange("p (h d) -> p h d", h=4)
-                nc.vector.tensor_tensor(out=o[:, :, 4 * g + j, :], in0=bank_v, in1=bias_v, op=ADD)
-                if r in V_SUM:
-                    dst = mean_tile(n)[:, :, q, :] if j == 3 else run[:]
+                bank = banks[j][:].rearrange("p (h d) -> p h d", h=4)
+                nc.vector.tensor_tensor(out=o[:, :, j, :], in0=bank, in1=bias_n, op=ADD)
+                if summed_on_vector(r):
                     nc.vector.scalar_tensor_tensor(
-                        out=dst, in0=bank_v, scalar=0.25, in1=(bias_v if j == 0 else run[:]), op0=MULT, op1=ADD
+                        out=(mean_tile(n)[:, :, q, :] if j == 3 else run[:]),
+                        in0=bank,
+                        scalar=0.25,
+                        in1=(bias_n if j == 0 else run[:]),
+                        op0=MULT,
+                        op1=ADD,
                     )
-                run_ops(V_IN.get((r, j), ()))
-            run_ops(AFTER.get(r, ()))
-            h0 = 4 * (n % 2)
-            if r >= 14:
-                nc.sync.dma_start(
-                    out=kv_views[n // 2][:, h0:h0 + 4, 512 * q:512 * (q + 1)],
-                    in_=o[:, :, 4 * g:4 * (g + 1), :].rearrange("p h j d -> p h (j d)"),
-                )
-            elif g == 1:
-                nc.sync.dma_start(
-                    out=kv_views[n // 2][:, h0:h0 + 4, 512 * (q - 1):512 * (q + 1)],
-                    in_=o[:].rearrange("p h j d -> p h (j d)"),
-                )
-            if r in V_SUM:
-                pending.append((r, r, "stored"))
-            else:
-                half = halfp.tile([P, 4, 2, P], F32)
-                nc.gpsimd.tensor_tensor(out=half[:], in0=o[:, :, 4 * g:4 * g + 2, :], in1=o[:, :, 4 * g + 2:4 * g + 4, :], op=ADD)
-                total = totalp.tile([P, 4, P], F32, tag="total")
+                if j == 1 and fresh is not None:
+                    quantise(fresh)
+            nc.sync.dma_start(
+                out=kv_views[n // 2][:, 4 * (n % 2):4 * (n % 2) + 4, BANK * q:BANK * (q + 1)],
+                in_=o[:].rearrange("p h j d -> p h (j d)"),
+            )
+            if not summed_on_vector(r):
+                half = half_pool.tile([P, 4, 2, P], F32)
+                nc.gpsimd.tensor_tensor(out=half[:], in0=o[:, :, 0:2, :], in1=o[:, :, 2:4, :], op=ADD)
+                total = total_pool.tile([P, 4, P], F32)
                 nc.gpsimd.tensor_tensor(out=total[:], in0=half[:, :, 0, :], in1=half[:, :, 1, :], op=ADD)
                 totals[r] = total
-                pending.append((min(15, r + SCALE_LAG), r, "scale"))
-            for due, rr, what in sorted(pending, key=lambda item: item[1]):
-                if due == r:
-                    if what == "scale":
-                        scale_round(rr)
-                    else:
-                        after_mean(rr)
+                waiting.append(r)
+            while scaled < len(waiting) and (waiting[scaled] + SCALE_LAG <= r or r == ROUNDS - 1):
+                scale(waiting[scaled])
+                scaled += 1

@@ -19,7 +19,7 @@ BANK = 512
 UNIT = 4096
 WORDS = UNIT // 4
 ROUNDS = 16
-SCALE_LAG = 3
+SCALE_LAG = 5
 
 
 def tile_chunkedattention_pb_kernel(tc, hidden_states, wk, bk, wv, bv, out_0, out_1, out_2, out_3):
@@ -36,13 +36,13 @@ def tile_chunkedattention_pb_kernel(tc, hidden_states, wk, bk, wv, bv, out_0, ou
         return i if kind == "x" else 4 * i
 
     def summed_on_vector(r):
-        return r % 4 == 3 and r > 3
+        return r in (9, 14, 15)
 
     with ExitStack() as ctx:
         const = ctx.enter_context(tc.tile_pool(name="const", bufs=1))
         raw_pool = ctx.enter_context(tc.tile_pool(name="raw_pool", bufs=4))
         grouped_pool = ctx.enter_context(tc.tile_pool(name="grouped_pool", bufs=3))
-        out_pool = ctx.enter_context(tc.tile_pool(name="out_pool", bufs=8))
+        out_pool = ctx.enter_context(tc.tile_pool(name="out_pool", bufs=9))
         half_pool = ctx.enter_context(tc.tile_pool(name="half_pool", bufs=2))
         total_pool = ctx.enter_context(tc.tile_pool(name="total_pool", bufs=SCALE_LAG + 2))
         run_pool = ctx.enter_context(tc.tile_pool(name="run_pool", bufs=2))
@@ -134,14 +134,19 @@ def tile_chunkedattention_pb_kernel(tc, hidden_states, wk, bk, wv, bv, out_0, ou
                 means[n] = mean_pool.tile([P, 4, 4, P], F32, name="mean")
             return means[n]
 
+        def store_means(n, q0, q1):
+            nc.scalar.dma_start(
+                out=mean_views[n // 2][:, 4 * (n % 2):4 * (n % 2) + 4, P * q0:P * q1],
+                in_=means[n][:, :, q0:q1, :].rearrange("p h q d -> p h (q d)"),
+            )
+
         def scale(r):
             n, q = divmod(r, 4)
             nc.scalar.activation(out=mean_tile(n)[:, :, q, :], in_=totals[r][:], func=COPY, scale=0.25)
-            if r == max(s for s in range(4 * n, 4 * n + 4) if not summed_on_vector(s)):
-                nc.scalar.dma_start(
-                    out=mean_views[n // 2][:, 4 * (n % 2):4 * (n % 2) + 4, :],
-                    in_=means[n][:].rearrange("p h q d -> p h (q d)"),
-                )
+            if n == 3:
+                store_means(n, q, q + 1)
+            elif r == max(s for s in range(4 * n, 4 * n + 4) if not summed_on_vector(s)):
+                store_means(n, 0, 4)
 
         waiting = []
         scaled = 0
@@ -188,10 +193,24 @@ def tile_chunkedattention_pb_kernel(tc, hidden_states, wk, bk, wv, bv, out_0, ou
                     )
                 if j == 1 and fresh is not None:
                     quantise(fresh)
-            nc.sync.dma_start(
-                out=kv_views[n // 2][:, 4 * (n % 2):4 * (n % 2) + 4, BANK * q:BANK * (q + 1)],
-                in_=o[:].rearrange("p h j d -> p h (j d)"),
-            )
+                if r == ROUNDS - 1 and j % 2 == 1:
+                    nc.sync.dma_start(
+                        out=kv_views[n // 2][:, 4 * (n % 2):4 * (n % 2) + 4, BANK * q + P * (j - 1):BANK * q + P * (j + 1)],
+                        in_=o[:, :, j - 1:j + 1, :].rearrange("p h j d -> p h (j d)"),
+                    )
+            if r == 14:
+                nc.sync.dma_start(
+                    out=mean_views[n // 2][:, 4 * (n % 2):4 * (n % 2) + 4, P * q:P * (q + 1)], in_=means[n][:, :, q, :]
+                )
+            if r < ROUNDS - 1:
+                nc.sync.dma_start(
+                    out=kv_views[n // 2][:, 4 * (n % 2):4 * (n % 2) + 4, BANK * q:BANK * (q + 1)],
+                    in_=o[:].rearrange("p h j d -> p h (j d)"),
+                )
+            else:
+                nc.sync.dma_start(
+                    out=mean_views[n // 2][:, 4 * (n % 2):4 * (n % 2) + 4, P * q:P * (q + 1)], in_=means[n][:, :, q, :]
+                )
             if not summed_on_vector(r):
                 half = half_pool.tile([P, 4, 2, P], F32)
                 nc.gpsimd.tensor_tensor(out=half[:], in0=o[:, :, 0:2, :], in1=o[:, :, 2:4, :], op=ADD)

@@ -19,7 +19,7 @@ BANK = 512
 UNIT = 4096
 WORDS = UNIT // 4
 ROUNDS = 16
-SCALE_LAG = 5
+SCALE_LAG = 3
 
 
 def tile_chunkedattention_pb_kernel(tc, hidden_states, wk, bk, wv, bv, out_0, out_1, out_2, out_3):
@@ -36,13 +36,13 @@ def tile_chunkedattention_pb_kernel(tc, hidden_states, wk, bk, wv, bv, out_0, ou
         return i if kind == "x" else 4 * i
 
     def summed_on_vector(r):
-        return r in (9, 14, 15)
+        return r % 4 == 3 and r > 3
 
     with ExitStack() as ctx:
         const = ctx.enter_context(tc.tile_pool(name="const", bufs=1))
         raw_pool = ctx.enter_context(tc.tile_pool(name="raw_pool", bufs=4))
         grouped_pool = ctx.enter_context(tc.tile_pool(name="grouped_pool", bufs=3))
-        out_pool = ctx.enter_context(tc.tile_pool(name="out_pool", bufs=9))
+        out_pool = ctx.enter_context(tc.tile_pool(name="out_pool", bufs=8))
         half_pool = ctx.enter_context(tc.tile_pool(name="half_pool", bufs=2))
         total_pool = ctx.enter_context(tc.tile_pool(name="total_pool", bufs=SCALE_LAG + 2))
         run_pool = ctx.enter_context(tc.tile_pool(name="run_pool", bufs=2))
@@ -71,7 +71,7 @@ def tile_chunkedattention_pb_kernel(tc, hidden_states, wk, bk, wv, bv, out_0, ou
         raws = {}
         groupeds = {}
 
-        def load(unit, pieces):
+        def load(unit):
             kind, i = unit
             raw = raw_pool.tile([P, UNIT], BF16)
             if kind == "x":
@@ -79,9 +79,8 @@ def tile_chunkedattention_pb_kernel(tc, hidden_states, wk, bk, wv, bv, out_0, ou
             else:
                 src = w_views[i // 2][:, i % 2]
             dst = raw[:].rearrange("p (f e) -> p f e", f=4)
-            step = 4 // pieces
-            for f in range(0, 4, step):
-                nc.sync.dma_start(out=dst[:, f:f + step, :], in_=src[:, f:f + step, :])
+            for f in (0, 2):
+                nc.sync.dma_start(out=dst[:, f:f + 2, :], in_=src[:, f:f + 2, :])
             raws[unit] = raw
 
         def transpose(unit, vector_helps):
@@ -113,12 +112,11 @@ def tile_chunkedattention_pb_kernel(tc, hidden_states, wk, bk, wv, bv, out_0, ou
                 in_=groupeds[unit][:],
             )
 
-        load(units[0], 2)
-        for unit in units[1:4]:
-            load(unit, 1)
+        for unit in units[0:4]:
+            load(unit)
         for k in range(2):
             transpose(units[k], True)
-            load(units[k + 4], 1)
+            load(units[k + 4])
             quantise(units[k])
         for n in range(4):
             spread = psum_m.tile([P, BANK], F32, tag="acc")
@@ -134,19 +132,14 @@ def tile_chunkedattention_pb_kernel(tc, hidden_states, wk, bk, wv, bv, out_0, ou
                 means[n] = mean_pool.tile([P, 4, 4, P], F32, name="mean")
             return means[n]
 
-        def store_means(n, q0, q1):
-            nc.scalar.dma_start(
-                out=mean_views[n // 2][:, 4 * (n % 2):4 * (n % 2) + 4, P * q0:P * q1],
-                in_=means[n][:, :, q0:q1, :].rearrange("p h q d -> p h (q d)"),
-            )
-
         def scale(r):
             n, q = divmod(r, 4)
             nc.scalar.activation(out=mean_tile(n)[:, :, q, :], in_=totals[r][:], func=COPY, scale=0.25)
-            if n == 3:
-                store_means(n, q, q + 1)
-            elif r == max(s for s in range(4 * n, 4 * n + 4) if not summed_on_vector(s)):
-                store_means(n, 0, 4)
+            if r == max(s for s in range(4 * n, 4 * n + 4) if not summed_on_vector(s)):
+                nc.scalar.dma_start(
+                    out=mean_views[n // 2][:, 4 * (n % 2):4 * (n % 2) + 4, :],
+                    in_=means[n][:].rearrange("p h q d -> p h (q d)"),
+                )
 
         waiting = []
         scaled = 0
@@ -157,13 +150,13 @@ def tile_chunkedattention_pb_kernel(tc, hidden_states, wk, bk, wv, bv, out_0, ou
                 fresh = units[prepared]
                 transpose(fresh, False)
                 if prepared + 4 < len(units):
-                    load(units[prepared + 4], 1)
+                    load(units[prepared + 4])
                 prepared += 1
             banks = []
-            for j in range(4):
+            for t in range(4):
                 acc = psum_m.tile([P, BANK], F32)
                 for s in range(2):
-                    xo = WORDS * q + 2 * P * j + P * s
+                    xo = WORDS * q + 2 * P * t + P * s
                     wo = WORDS * n + BANK * s
                     nc.tensor.matmul_mx(
                         out=acc[:],
@@ -179,38 +172,24 @@ def tile_chunkedattention_pb_kernel(tc, hidden_states, wk, bk, wv, bv, out_0, ou
             bias_n = bias[:, BANK * n:BANK * (n + 1)].rearrange("p (h d) -> p h d", h=4)
             if summed_on_vector(r):
                 run = run_pool.tile([P, 4, P], F32)
-            for j in range(4):
-                bank = banks[j][:].rearrange("p (h d) -> p h d", h=4)
-                nc.vector.tensor_tensor(out=o[:, :, j, :], in0=bank, in1=bias_n, op=ADD)
+            for t in range(4):
+                bank = banks[t][:].rearrange("p (h d) -> p h d", h=4)
+                nc.vector.tensor_tensor(out=o[:, :, t, :], in0=bank, in1=bias_n, op=ADD)
                 if summed_on_vector(r):
                     nc.vector.scalar_tensor_tensor(
-                        out=(mean_tile(n)[:, :, q, :] if j == 3 else run[:]),
+                        out=(mean_tile(n)[:, :, q, :] if t == 3 else run[:]),
                         in0=bank,
                         scalar=0.25,
-                        in1=(bias_n if j == 0 else run[:]),
+                        in1=(bias_n if t == 0 else run[:]),
                         op0=MULT,
                         op1=ADD,
                     )
-                if j == 1 and fresh is not None:
+                if t == 1 and fresh is not None:
                     quantise(fresh)
-                if r == ROUNDS - 1 and j % 2 == 1:
-                    nc.sync.dma_start(
-                        out=kv_views[n // 2][:, 4 * (n % 2):4 * (n % 2) + 4, BANK * q + P * (j - 1):BANK * q + P * (j + 1)],
-                        in_=o[:, :, j - 1:j + 1, :].rearrange("p h j d -> p h (j d)"),
-                    )
-            if r == 14:
-                nc.sync.dma_start(
-                    out=mean_views[n // 2][:, 4 * (n % 2):4 * (n % 2) + 4, P * q:P * (q + 1)], in_=means[n][:, :, q, :]
-                )
-            if r < ROUNDS - 1:
-                nc.sync.dma_start(
-                    out=kv_views[n // 2][:, 4 * (n % 2):4 * (n % 2) + 4, BANK * q:BANK * (q + 1)],
-                    in_=o[:].rearrange("p h j d -> p h (j d)"),
-                )
-            else:
-                nc.sync.dma_start(
-                    out=mean_views[n // 2][:, 4 * (n % 2):4 * (n % 2) + 4, P * q:P * (q + 1)], in_=means[n][:, :, q, :]
-                )
+            nc.sync.dma_start(
+                out=kv_views[n // 2][:, 4 * (n % 2):4 * (n % 2) + 4, BANK * q:BANK * (q + 1)],
+                in_=o[:].rearrange("p h j d -> p h (j d)"),
+            )
             if not summed_on_vector(r):
                 half = half_pool.tile([P, 4, 2, P], F32)
                 nc.gpsimd.tensor_tensor(out=half[:], in0=o[:, :, 0:2, :], in1=o[:, :, 2:4, :], op=ADD)

from contextlib import ExitStack

import concourse.mybir as mybir
from concourse.masks import make_identity

F32 = mybir.dt.float32
BF16 = mybir.dt.bfloat16
U32 = mybir.dt.uint32
U8 = mybir.dt.uint8
FP8X4 = mybir.dt.float8_e4m3fn_x4
ADD = mybir.AluOpType.add
MULT = mybir.AluOpType.mult
COPY = mybir.ActivationFunctionType.Copy

FLOPS = 2 * 2048 * 1024 * 2048

P = 128
BANK = 512
UNIT = 4096
WORDS = UNIT // 4
ROUNDS = 16
SCALE_LAG = 3


def tile_chunkedattention_pb_kernel(tc, hidden_states, wk, bk, wv, bv, out_0, out_1, out_2, out_3):
    nc = tc.nc
    x_view = hidden_states.flatten_outer_dims().rearrange("(p q t) e -> p q (t e)", p=P, q=4, t=4)
    w_views = [w.rearrange("(n f p) e -> p n f e", n=2, f=4, p=P) for w in (wk, wv)]
    kv_views = [o.rearrange("b h (p q) t d -> p (b h) (q t d)", p=P, q=4) for o in (out_0, out_1)]
    mean_views = [o.rearrange("b h (p q) d -> p (b h) (q d)", p=P, q=4) for o in (out_2, out_3)]

    units = [("w", 0), ("x", 0), ("x", 1), ("x", 2), ("x", 3), ("w", 1), ("w", 2), ("w", 3)]

    def first_round(unit):
        kind, i = unit
        return i if kind == "x" else 4 * i

    def summed_on_vector(r):
        return r % 4 == 3 and r > 3

    with ExitStack() as ctx:
        const = ctx.enter_context(tc.tile_pool(name="const", bufs=1))
        raw_pool = ctx.enter_context(tc.tile_pool(name="raw_pool", bufs=4))
        grouped_pool = ctx.enter_context(tc.tile_pool(name="grouped_pool", bufs=3))
        out_pool = ctx.enter_context(tc.tile_pool(name="out_pool", bufs=8))
        half_pool = ctx.enter_context(tc.tile_pool(name="half_pool", bufs=2))
        total_pool = ctx.enter_context(tc.tile_pool(name="total_pool", bufs=SCALE_LAG + 2))
        run_pool = ctx.enter_context(tc.tile_pool(name="run_pool", bufs=2))
        mean_pool = ctx.enter_context(tc.tile_pool(name="mean_pool", bufs=2))
        psum_t = ctx.enter_context(tc.psum_pool(name="psum_t", bufs=4))
        psum_m = ctx.enter_context(tc.psum_pool(name="psum_m", bufs=4))
        ctx.enter_context(tc.manual_schedule())

        ident = const.tile([P, P], F32)
        make_identity(nc, ident[:])
        ones = const.tile([P, P], BF16)
        nc.vector.memset(ones[:], 1.0)
        bias_rows = const.tile([P, 4 * BANK], BF16)
        nc.vector.memset(bias_rows[:], 0.0)
        nc.scalar.dma_start(out=bias_rows[0:1, 0:2 * BANK], in_=bk.unsqueeze(0))
        nc.scalar.dma_start(out=bias_rows[0:1, 2 * BANK:4 * BANK], in_=bv.unsqueeze(0))
        bias = const.tile([P, 4 * BANK], F32)
        codes = {
            "x": const.tile([P, 4 * WORDS], U32, align_bytes=64, name="x_codes"),
            "w": const.tile([P, 4 * WORDS], U32, align_bytes=64, name="w_codes"),
        }
        scales = {
            "x": const.tile([P, 4 * WORDS], U8, align_bytes=64, name="x_scales"),
            "w": const.tile([P, 4 * WORDS], U8, align_bytes=64, name="w_scales"),
        }
        raws = {}
        groupeds = {}

        def load(unit):
            kind, i = unit
            raw = raw_pool.tile([P, UNIT], BF16)
            if kind == "x":
                src = x_view[:, i, :].rearrange("p (f e) -> p f e", f=4)
            else:
                src = w_views[i // 2][:, i % 2]
            dst = raw[:].rearrange("p (f e) -> p f e", f=4)
            for f in (0, 2):
                nc.sync.dma_start(out=dst[:, f:f + 2, :], in_=src[:, f:f + 2, :])
            raws[unit] = raw

        def transpose(unit, vector_helps):
            kind = unit[0]
            raw_words = raws[unit][:].bitcast(F32)
            grouped = grouped_pool.tile([P, UNIT], BF16, align_bytes=64)
            grouped_words = grouped[:].bitcast(F32)
            if kind == "x":
                dst = grouped_words.rearrange("p (f s c u) -> p f s c u", f=4, s=2, c=P, u=2)
            else:
                dst = grouped_words.rearrange("p (s f c u) -> p f s c u", s=2, f=4, c=P, u=2)
            for f in range(4):
                turned = psum_t.tile([P, BANK], F32)
                for a in range(4):
                    lo = BANK * f + P * a
                    nc.tensor.transpose(turned[:, P * a:P * (a + 1)], raw_words[:, lo:lo + P], ident[:])
                src = turned[:].rearrange("p (s u c) -> p s c u", s=2, u=2, c=P)
                if vector_helps and f % 2 == 1:
                    nc.vector.tensor_copy(out=dst[:, f], in_=src)
                else:
                    nc.scalar.copy(out=dst[:, f], in_=src)
            groupeds[unit] = grouped

        def quantise(unit):
            kind, i = unit
            nc.vector.quantize_mx(
                out=codes[kind][:, WORDS * i:WORDS * (i + 1)].bitcast(FP8X4),
                scales=scales[kind][:, WORDS * i:WORDS * (i + 1)],
                in_=groupeds[unit][:],
            )

        for unit in units[0:4]:
            load(unit)
        for k in range(2):
            transpose(units[k], True)
            load(units[k + 4])
            quantise(units[k])
        for n in range(4):
            spread = psum_m.tile([P, BANK], F32, tag="acc")
            nc.tensor.matmul(out=spread[:], lhsT=ones[:], rhs=bias_rows[:, BANK * n:BANK * (n + 1)], start=True, stop=True)
            nc.vector.tensor_copy(out=bias[:, BANK * n:BANK * (n + 1)], in_=spread[:])
        prepared = 2

        totals = {}
        means = {}

        def mean_tile(n):
            if n not in means:
                means[n] = mean_pool.tile([P, 4, 4, P], F32, name="mean")
            return means[n]

        def scale(r):
            n, q = divmod(r, 4)
            nc.scalar.activation(out=mean_tile(n)[:, :, q, :], in_=totals[r][:], func=COPY, scale=0.25)
            if r == max(s for s in range(4 * n, 4 * n + 4) if not summed_on_vector(s)):
                nc.scalar.dma_start(
                    out=mean_views[n // 2][:, 4 * (n % 2):4 * (n % 2) + 4, :],
                    in_=means[n][:].rearrange("p h q d -> p h (q d)"),
                )

        waiting = []
        scaled = 0
        for r in range(ROUNDS):
            n, q = divmod(r, 4)
            fresh = None
            if prepared < len(units) and r == first_round(units[prepared - 1]):
                fresh = units[prepared]
                transpose(fresh, False)
                if prepared + 4 < len(units):
                    load(units[prepared + 4])
                prepared += 1
            banks = []
            for t in range(4):
                acc = psum_m.tile([P, BANK], F32)
                for s in range(2):
                    xo = WORDS * q + 2 * P * t + P * s
                    wo = WORDS * n + BANK * s
                    nc.tensor.matmul_mx(
                        out=acc[:],
                        lhsT=codes["x"][:, xo:xo + P].bitcast(FP8X4),
                        lhsT_scale=scales["x"][:, xo:xo + P],
                        rhs=codes["w"][:, wo:wo + BANK].bitcast(FP8X4),
                        rhs_scale=scales["w"][:, wo:wo + BANK],
                        start=(s == 0),
                        stop=(s == 1),
                    )
                banks.append(acc)
            o = out_pool.tile([P, 4, 4, P], F32)
            bias_n = bias[:, BANK * n:BANK * (n + 1)].rearrange("p (h d) -> p h d", h=4)
            if summed_on_vector(r):
                run = run_pool.tile([P, 4, P], F32)
            for t in range(4):
                bank = banks[t][:].rearrange("p (h d) -> p h d", h=4)
                nc.vector.tensor_tensor(out=o[:, :, t, :], in0=bank, in1=bias_n, op=ADD)
                if summed_on_vector(r):
                    nc.vector.scalar_tensor_tensor(
                        out=(mean_tile(n)[:, :, q, :] if t == 3 else run[:]),
                        in0=bank,
                        scalar=0.25,
                        in1=(bias_n if t == 0 else run[:]),
                        op0=MULT,
                        op1=ADD,
                    )
                if t == 1 and fresh is not None:
                    quantise(fresh)
            nc.sync.dma_start(
                out=kv_views[n // 2][:, 4 * (n % 2):4 * (n % 2) + 4, BANK * q:BANK * (q + 1)],
                in_=o[:].rearrange("p h j d -> p h (j d)"),
            )
            if not summed_on_vector(r):
                half = half_pool.tile([P, 4, 2, P], F32)
                nc.gpsimd.tensor_tensor(out=half[:], in0=o[:, :, 0:2, :], in1=o[:, :, 2:4, :], op=ADD)
                total = total_pool.tile([P, 4, P], F32)
                nc.gpsimd.tensor_tensor(out=total[:], in0=half[:, :, 0, :], in1=half[:, :, 1, :], op=ADD)
                totals[r] = total
                waiting.append(r)
            while scaled < len(waiting) and (waiting[scaled] + SCALE_LAG <= r or r == ROUNDS - 1):
                scale(waiting[scaled])
                scaled += 1
